import numpy as np
import ml_dtypes


def mxq(x, axis, fmt="e4m3"):
    dtype, down = {"e4m3": (ml_dtypes.float8_e4m3fn, 7), "e5m2": (ml_dtypes.float8_e5m2, 14)}[fmt]
    v = np.moveaxis(np.asarray(x, np.float32).astype(ml_dtypes.bfloat16).astype(np.float64), axis, -1)
    blocks = v.reshape(v.shape[:-1] + (-1, 32))
    amax = np.abs(blocks).max(-1, keepdims=True)
    byte = np.maximum(np.where(amax > 0, np.frexp(amax)[1] - 1 + 127, 0) - down, 1)
    scale = np.exp2(byte - 127.0)
    codes = (blocks / scale).astype(np.float32).astype(dtype).astype(np.float64)
    return np.moveaxis((codes * scale).reshape(v.shape), -1, axis)


WIDE = False


def mx_kscale(k):
    if not WIDE:
        return np.ones(k)
    levels = np.array([20, -20, 10, -10, 0])
    a = np.random.permutation(np.resize(levels, k // 512 * 4)).reshape(k // 512, 4)
    idx = np.arange(k)
    return np.exp2(a[idx // 512, idx % 128 // 32])


BF16 = ml_dtypes.bfloat16


def bf(x):
    return np.asarray(x, np.float32).astype(BF16)


def f64(x):
    return np.asarray(x).astype(np.float64)


N, H, W, K = 2048, 512, 2, 1024
TAU = 1.0


def sigmoid(v):
    return 1.0 / (1.0 + np.exp(-v))


def softmax_first(v):
    e = np.exp(v - v.max(0, keepdims=True))
    return e / e.sum(0, keepdims=True)


def setup_inputs():
    u = mx_kscale(H)
    x = bf(np.random.standard_normal((N, W * K)))
    t0 = bf(np.random.standard_normal((H, W * K)) / np.sqrt(K))
    g = bf(np.random.standard_normal((N, H)) * np.exp2(np.random.randint(-12, 1, (N, 1))) * 8.0 * u)
    xw = f64(x).reshape(N, W, K).transpose(1, 0, 2)
    tw = f64(t0).reshape(H, W, K).transpose(1, 2, 0)
    s = xw @ tw
    return {"x": x, "template_flat": bf(f64(t0) / u[:, None]), "s": np.asarray(s, np.float32), "grad_out": g}


def reference(x, template_flat, s, grad_out):
    sf = f64(s)
    gate = softmax_first(sf / TAU)
    sg = sigmoid(sf)
    f = sf * sg
    df = sg * (1.0 + sf * (1.0 - sg))
    y = np.sum(gate * f, axis=0, keepdims=True)
    ds = f64(grad_out)[None, :, :] * gate * (df + (f - y) / TAU)
    tw = f64(template_flat).reshape(H, W, K).transpose(1, 0, 2)
    dx = mxq(ds, 2, "e5m2") @ mxq(tw, 1, "e4m3")
    return dx.transpose(1, 0, 2).reshape(N, W * K)

@@ -1,0 +1,229 @@
+from contextlib import ExitStack
+
+import concourse.mybir as mybir
+from concourse.masks import make_identity
+
+F32 = mybir.dt.float32
+BF16 = mybir.dt.bfloat16
+U32 = mybir.dt.uint32
+U8 = mybir.dt.uint8
+E5M2_X4 = mybir.dt.float8_e5m2_x4
+E4M3_X4 = mybir.dt.float8_e4m3fn_x4
+ALU = mybir.AluOpType
+ACT = mybir.ActivationFunctionType
+
+P = 128
+PACK = 4
+N_ROWS = 2048
+H = P * PACK
+W = 2
+K = 1024
+N_MX = 512
+ROW_TILES = N_ROWS // P
+CHUNK = 2
+CHUNKS = ROW_TILES // CHUNK
+CW = CHUNK * H
+BRACKET_TO_DS = (-0.25, 0.25)
+
+FLOPS = 2 * W * N_ROWS * H * K
+BYTES = 2 * H * W * K + 4 * W * N_ROWS * H + 2 * N_ROWS * H + 4 * N_ROWS * W * K
+
+
+def tile_dendriticlayersilu_ffn_t_v_kernel(tc, x, template_flat, s, grad_out, out):
+    nc = tc.nc
+
+    s_view = s.rearrange("w (p t) h -> p w t h", t=ROW_TILES)
+    g_view = grad_out.rearrange("(p t) h -> p t h", t=ROW_TILES)
+    out_view = out.rearrange("(p t) c -> p t c", t=ROW_TILES)
+    template_view = template_flat.rearrange("(j p) c -> p j c", p=P)
+
+    with ExitStack() as stack:
+        const = stack.enter_context(tc.tile_pool(name="const", bufs=1))
+        loads = stack.enter_context(tc.tile_pool(name="loads", bufs=4))
+        work = stack.enter_context(tc.tile_pool(name="work", bufs=2))
+        turned = stack.enter_context(tc.tile_pool(name="turned", bufs=2))
+        stores = stack.enter_context(tc.tile_pool(name="stores", bufs=3))
+        psum_bracket = stack.enter_context(tc.psum_pool(name="psum_bracket", bufs=CHUNK * W))
+        psum_grad = stack.enter_context(tc.psum_pool(name="psum_grad", bufs=1))
+        psum_out = stack.enter_context(tc.psum_pool(name="psum_out", bufs=3))
+        stack.enter_context(tc.manual_schedule())
+
+        ident_f32 = const.tile([P, P], F32)
+        make_identity(nc, ident_f32[:])
+        ident_bf16 = const.tile([P, P], BF16)
+        make_identity(nc, ident_bf16[:])
+
+        template_raw = const.tile([P, PACK, W * K], BF16)
+        template_grouped = const.tile([P, W * K, PACK], BF16, align_bytes=64)
+        template_codes = const.tile([P, W * K], U32, align_bytes=64)
+        template_scales = const.tile([P, W * K], U8, align_bytes=64)
+
+        def load_template(w):
+            cols = slice(w * K, (w + 1) * K)
+            nc.sync.dma_start(out=template_raw[:, :, cols], in_=template_view[:, :, cols])
+
+        def group_template(w):
+            cols = slice(w * K, (w + 1) * K)
+            nc.vector.tensor_copy(
+                out=template_grouped[:, cols, :].rearrange("p (c i) j -> p c j i", i=4),
+                in_=template_raw[:, :, cols].rearrange("p j (c i) -> p c j i", i=4),
+            )
+
+        def quantise_template(w):
+            cols = slice(w * K, (w + 1) * K)
+            nc.vector.quantize_mx(
+                out=template_codes[:, cols].bitcast(E4M3_X4),
+                scales=template_scales[:, cols],
+                in_=template_grouped[:, cols, :].rearrange("p c j -> p (c j)"),
+            )
+
+        def load_chunk(c):
+            tiles = slice(c * CHUNK, (c + 1) * CHUNK)
+            s_sb = loads.tile([P, W, CW], F32)
+            nc.sync.dma_start(out=s_sb[:].rearrange("p w (t h) -> p w t h", h=H), in_=s_view[:, :, tiles, :])
+            g_sb = loads.tile([P, CHUNK, H], BF16)
+            nc.sync.dma_start(out=g_sb[:], in_=g_view[:, tiles, :])
+            return {"s": s_sb, "g": g_sb}
+
+        def activations(chunk):
+            s_sb = chunk["s"]
+            n_t = work.tile([P, W, CW], F32)
+            f_t = work.tile([P, W, CW], F32)
+            z_t = work.tile([P, CW], F32)
+            zz_t = work.tile([P, CW], F32)
+            nc.vector.tensor_tensor(out=z_t[:], in0=s_sb[:, 0, :], in1=s_sb[:, 1, :], op=ALU.subtract)
+            nc.scalar.activation(out=n_t[:], in_=s_sb[:], func=ACT.Tanh, scale=0.5)
+            nc.scalar.activation(out=f_t[:], in_=s_sb[:], func=ACT.Silu)
+            nc.scalar.activation(out=z_t[:], in_=z_t[:], func=ACT.Tanh, scale=0.5)
+            nc.scalar.activation(out=zz_t[:], in_=z_t[:], func=ACT.Square)
+            chunk["n"] = n_t
+            chunk["f"] = f_t
+            chunk["z"] = z_t
+            chunk["zz"] = zz_t
+
+        def slopes(chunk):
+            n_t, f_t = chunk["n"], chunk["f"]
+            shared_t = work.tile([P, CW], F32)
+            nc.vector.scalar_tensor_tensor(
+                out=n_t[:], in0=f_t[:], scalar=1.0, in1=n_t[:], op0=ALU.subtract, op1=ALU.mult
+            )
+            nc.vector.tensor_tensor(out=shared_t[:], in0=f_t[:, 0, :], in1=f_t[:, 1, :], op=ALU.subtract)
+            nc.vector.scalar_tensor_tensor(
+                out=n_t[:], in0=n_t[:], scalar=1.0, in1=f_t[:], op0=ALU.subtract, op1=ALU.subtract
+            )
+            chunk["shared"] = shared_t
+
+        def bracket_terms(chunk):
+            n_t, z_t, shared_t = chunk["n"], chunk["z"], chunk["shared"]
+            own_t = work.tile([P, W, CW], F32)
+            nc.vector.scalar_tensor_tensor(
+                out=shared_t[:], in0=chunk["zz"][:], scalar=1.0, in1=shared_t[:], op0=ALU.subtract, op1=ALU.mult
+            )
+            nc.vector.scalar_tensor_tensor(
+                out=own_t[:, 0, :], in0=z_t[:], scalar=1.0, in1=n_t[:, 0, :], op0=ALU.add, op1=ALU.mult
+            )
+            nc.vector.scalar_tensor_tensor(
+                out=own_t[:, 1, :], in0=z_t[:], scalar=1.0, in1=n_t[:, 1, :], op0=ALU.subtract, op1=ALU.mult
+            )
+            chunk["own"] = own_t
+
+        def turn(chunk):
+            g_ps = psum_grad.tile([P, CHUNK, PACK, P], BF16)
+            for local in range(CHUNK):
+                for j in range(PACK):
+                    nc.tensor.transpose(
+                        out=g_ps[:, local, j, :], in_=chunk["g"][:, local, j * P : (j + 1) * P], identity=ident_bf16[:]
+                    )
+            chunk["brackets"] = []
+            for local in range(CHUNK):
+                for w in range(W):
+                    bracket_ps = psum_bracket.tile([P, PACK, P], F32)
+                    for j in range(PACK):
+                        block = slice(local * H + j * P, local * H + (j + 1) * P)
+                        nc.tensor.matmul(
+                            out=bracket_ps[:, j, :], lhsT=chunk["own"][:, w, block], rhs=ident_f32[:],
+                            is_transpose=True, start=True, stop=False,
+                        )
+                        nc.tensor.matmul(
+                            out=bracket_ps[:, j, :], lhsT=chunk["shared"][:, block], rhs=ident_f32[:],
+                            is_transpose=True, start=False, stop=True,
+                        )
+                    chunk["brackets"].append(bracket_ps)
+            chunk["g_ps"] = g_ps
+
+        def group_grad(chunk):
+            g_turned = turned.tile([P, CHUNK, P, PACK], BF16)
+            nc.scalar.copy(out=g_turned[:], in_=chunk["g_ps"][:].rearrange("p t j m -> p t m j"))
+            chunk["g_turned"] = g_turned
+
+        def quantise_ds(chunk):
+            ds_bf16 = turned.tile([P, CHUNK, W, P, PACK], BF16, align_bytes=64)
+            ds_codes = turned.tile([P, CHUNK, W * P], U32, align_bytes=64)
+            ds_scales = turned.tile([P, CHUNK, W * P], U8, align_bytes=64)
+            for local in range(CHUNK):
+                for w in range(W):
+                    nc.vector.scalar_tensor_tensor(
+                        out=ds_bf16[:, local, w],
+                        in0=chunk["brackets"][local * W + w][:].rearrange("p j m -> p m j"),
+                        scalar=BRACKET_TO_DS[w],
+                        in1=chunk["g_turned"][:, local],
+                        op0=ALU.mult,
+                        op1=ALU.mult,
+                    )
+            for local in range(CHUNK):
+                nc.vector.quantize_mx(
+                    out=ds_codes[:, local, :].bitcast(E5M2_X4),
+                    scales=ds_scales[:, local, :],
+                    in_=ds_bf16[:, local].rearrange("p w m j -> p (w m j)"),
+                )
+            chunk["ds_codes"] = ds_codes
+            chunk["ds_scales"] = ds_scales
+
+        def multiply_and_store(chunk, c):
+            for local in range(CHUNK):
+                out_sb = stores.tile([P, W * K], F32)
+                for w in range(W):
+                    rows = slice(w * P, (w + 1) * P)
+                    for c0 in range(w * K, (w + 1) * K, N_MX):
+                        cols = slice(c0, c0 + N_MX)
+                        acc = psum_out.tile([P, N_MX], F32)
+                        nc.tensor.matmul_mx(
+                            out=acc[:],
+                            lhsT=chunk["ds_codes"][:, local, rows].bitcast(E5M2_X4),
+                            lhsT_scale=chunk["ds_scales"][:, local, rows],
+                            rhs=template_codes[:, cols].bitcast(E4M3_X4),
+                            rhs_scale=template_scales[:, cols],
+                            start=True,
+                            stop=True,
+                        )
+                        nc.scalar.copy(out=out_sb[:, cols], in_=acc[:])
+                nc.scalar.dma_start(out=out_view[:, c * CHUNK + local, :], in_=out_sb[:])
+
+        load_template(0)
+        chunks = [load_chunk(0)]
+        load_template(1)
+        chunks.append(load_chunk(1))
+        chunks.append(load_chunk(2))
+
+        group_template(0)
+        activations(chunks[0])
+        quantise_template(0)
+        group_template(1)
+        activations(chunks[1])
+        quantise_template(1)
+        slopes(chunks[0])
+        bracket_terms(chunks[0])
+
+        for c in range(CHUNKS):
+            if c + 3 < CHUNKS:
+                chunks.append(load_chunk(c + 3))
+            turn(chunks[c])
+            if c + 2 < CHUNKS:
+                activations(chunks[c + 2])
+            group_grad(chunks[c])
+            if c + 1 < CHUNKS:
+                slopes(chunks[c + 1])
+            quantise_ds(chunks[c])
+            multiply_and_store(chunks[c], c)
+            if c + 1 < CHUNKS:
+                bracket_terms(chunks[c + 1])

@@ -39,10 +39,11 @@ def tile_dendriticlayersilu_ffn_t_v_kernel(tc, x, template_flat, s, grad_out, ou
 
     with ExitStack() as stack:
         const = stack.enter_context(tc.tile_pool(name="const", bufs=1))
+        template = stack.enter_context(tc.tile_pool(name="template", bufs=W * K // N_MX))
         loads = stack.enter_context(tc.tile_pool(name="loads", bufs=4))
         work = stack.enter_context(tc.tile_pool(name="work", bufs=2))
         turned = stack.enter_context(tc.tile_pool(name="turned", bufs=2))
-        stores = stack.enter_context(tc.tile_pool(name="stores", bufs=3))
+        stores = stack.enter_context(tc.tile_pool(name="stores", bufs=6))
         psum_bracket = stack.enter_context(tc.psum_pool(name="psum_bracket", bufs=CHUNK * W))
         psum_grad = stack.enter_context(tc.psum_pool(name="psum_grad", bufs=1))
         psum_out = stack.enter_context(tc.psum_pool(name="psum_out", bufs=3))
@@ -53,28 +54,28 @@ def tile_dendriticlayersilu_ffn_t_v_kernel(tc, x, template_flat, s, grad_out, ou
         ident_bf16 = const.tile([P, P], BF16)
         make_identity(nc, ident_bf16[:])
 
-        template_raw = const.tile([P, PACK, W * K], BF16)
-        template_grouped = const.tile([P, W * K, PACK], BF16, align_bytes=64)
         template_codes = const.tile([P, W * K], U32, align_bytes=64)
         template_scales = const.tile([P, W * K], U8, align_bytes=64)
 
-        def load_template(w):
-            cols = slice(w * K, (w + 1) * K)
-            nc.sync.dma_start(out=template_raw[:, :, cols], in_=template_view[:, :, cols])
+        def load_template(piece):
+            raw = template.tile([P, PACK, N_MX], BF16)
+            nc.sync.dma_start(out=raw[:], in_=template_view[:, :, piece * N_MX : (piece + 1) * N_MX])
+            return raw
 
-        def group_template(w):
-            cols = slice(w * K, (w + 1) * K)
+        def group_template(raw):
+            grouped = template.tile([P, N_MX, PACK], BF16, align_bytes=64)
             nc.vector.tensor_copy(
-                out=template_grouped[:, cols, :].rearrange("p (c i) j -> p c j i", i=4),
-                in_=template_raw[:, :, cols].rearrange("p j (c i) -> p c j i", i=4),
+                out=grouped[:].rearrange("p (c i) j -> p c j i", i=4),
+                in_=raw[:].rearrange("p j (c i) -> p c j i", i=4),
             )
+            return grouped
 
-        def quantise_template(w):
-            cols = slice(w * K, (w + 1) * K)
+        def quantise_template(piece, grouped):
+            cols = slice(piece * N_MX, (piece + 1) * N_MX)
             nc.vector.quantize_mx(
                 out=template_codes[:, cols].bitcast(E4M3_X4),
                 scales=template_scales[:, cols],
-                in_=template_grouped[:, cols, :].rearrange("p c j -> p (c j)"),
+                in_=grouped[:].rearrange("p c j -> p (c j)"),
             )
 
         def load_chunk(c):
@@ -127,13 +128,16 @@ def tile_dendriticlayersilu_ffn_t_v_kernel(tc, x, template_flat, s, grad_out, ou
             )
             chunk["own"] = own_t
 
-        def turn(chunk):
+        def turn_grad(chunk):
             g_ps = psum_grad.tile([P, CHUNK, PACK, P], BF16)
             for local in range(CHUNK):
                 for j in range(PACK):
                     nc.tensor.transpose(
                         out=g_ps[:, local, j, :], in_=chunk["g"][:, local, j * P : (j + 1) * P], identity=ident_bf16[:]
                     )
+            chunk["g_ps"] = g_ps
+
+        def turn_brackets(chunk):
             chunk["brackets"] = []
             for local in range(CHUNK):
                 for w in range(W):
@@ -149,7 +153,6 @@ def tile_dendriticlayersilu_ffn_t_v_kernel(tc, x, template_flat, s, grad_out, ou
                             is_transpose=True, start=False, stop=True,
                         )
                     chunk["brackets"].append(bracket_ps)
-            chunk["g_ps"] = g_ps
 
         def group_grad(chunk):
             g_turned = turned.tile([P, CHUNK, P, PACK], BF16)
@@ -181,11 +184,11 @@ def tile_dendriticlayersilu_ffn_t_v_kernel(tc, x, template_flat, s, grad_out, ou
 
         def multiply_and_store(chunk, c):
             for local in range(CHUNK):
-                out_sb = stores.tile([P, W * K], F32)
                 for w in range(W):
                     rows = slice(w * P, (w + 1) * P)
-                    for c0 in range(w * K, (w + 1) * K, N_MX):
-                        cols = slice(c0, c0 + N_MX)
+                    out_sb = stores.tile([P, K], F32)
+                    for k0 in range(0, K, N_MX):
+                        cols = slice(w * K + k0, w * K + k0 + N_MX)
                         acc = psum_out.tile([P, N_MX], F32)
                         nc.tensor.matmul_mx(
                             out=acc[:],
@@ -196,32 +199,40 @@ def tile_dendriticlayersilu_ffn_t_v_kernel(tc, x, template_flat, s, grad_out, ou
                             start=True,
                             stop=True,
                         )
-                        nc.scalar.copy(out=out_sb[:, cols], in_=acc[:])
-                nc.scalar.dma_start(out=out_view[:, c * CHUNK + local, :], in_=out_sb[:])
+                        nc.scalar.copy(out=out_sb[:, k0 : k0 + N_MX], in_=acc[:])
+                    nc.scalar.dma_start(out=out_view[:, c * CHUNK + local, w * K : (w + 1) * K], in_=out_sb[:])
 
-        load_template(0)
+        raw_pieces = [load_template(0), load_template(1)]
         chunks = [load_chunk(0)]
-        load_template(1)
+        raw_pieces.append(load_template(2))
+        raw_pieces.append(load_template(3))
         chunks.append(load_chunk(1))
         chunks.append(load_chunk(2))
 
-        group_template(0)
+        grouped_pieces = [group_template(raw_pieces[0]), group_template(raw_pieces[1])]
+        quantise_template(0, grouped_pieces[0])
         activations(chunks[0])
-        quantise_template(0)
-        group_template(1)
+        quantise_template(1, grouped_pieces[1])
+        grouped_pieces.append(group_template(raw_pieces[2]))
+        grouped_pieces.append(group_template(raw_pieces[3]))
+        quantise_template(2, grouped_pieces[2])
         activations(chunks[1])
-        quantise_template(1)
+        quantise_template(3, grouped_pieces[3])
+        turn_grad(chunks[0])
+        group_grad(chunks[0])
         slopes(chunks[0])
         bracket_terms(chunks[0])
 
         for c in range(CHUNKS):
             if c + 3 < CHUNKS:
                 chunks.append(load_chunk(c + 3))
-            turn(chunks[c])
+            turn_brackets(chunks[c])
+            if c + 1 < CHUNKS:
+                turn_grad(chunks[c + 1])
             if c + 2 < CHUNKS:
                 activations(chunks[c + 2])
-            group_grad(chunks[c])
             if c + 1 < CHUNKS:
+                group_grad(chunks[c + 1])
                 slopes(chunks[c + 1])
             quantise_ds(chunks[c])
             multiply_and_store(chunks[c], c)

@@ -84,22 +84,27 @@ def tile_dendriticlayersilu_ffn_t_v_kernel(tc, x, template_flat, s, grad_out, ou
             nc.sync.dma_start(out=s_sb[:].rearrange("p w (t h) -> p w t h", h=H), in_=s_view[:, :, tiles, :])
             g_sb = loads.tile([P, CHUNK, H], BF16)
             nc.sync.dma_start(out=g_sb[:], in_=g_view[:, tiles, :])
-            return {"s": s_sb, "g": g_sb}
+            chunk = {"s": s_sb, "g": g_sb}
+            window_difference(chunk)
+            return chunk
+
+        def window_difference(chunk):
+            s_sb = chunk["s"]
+            z_t = work.tile([P, CW], F32, bufs=3)
+            nc.gpsimd.tensor_tensor(out=z_t[:], in0=s_sb[:, 0, :], in1=s_sb[:, 1, :], op=ALU.subtract)
+            chunk["z"] = z_t
 
         def activations(chunk):
-            s_sb = chunk["s"]
+            s_sb, z_t = chunk["s"], chunk["z"]
             n_t = work.tile([P, W, CW], F32)
             f_t = work.tile([P, W, CW], F32)
-            z_t = work.tile([P, CW], F32)
             zz_t = work.tile([P, CW], F32)
-            nc.vector.tensor_tensor(out=z_t[:], in0=s_sb[:, 0, :], in1=s_sb[:, 1, :], op=ALU.subtract)
             nc.scalar.activation(out=n_t[:], in_=s_sb[:], func=ACT.Tanh, scale=0.5)
             nc.scalar.activation(out=f_t[:], in_=s_sb[:], func=ACT.Silu)
             nc.scalar.activation(out=z_t[:], in_=z_t[:], func=ACT.Tanh, scale=0.5)
             nc.scalar.activation(out=zz_t[:], in_=z_t[:], func=ACT.Square)
             chunk["n"] = n_t
             chunk["f"] = f_t
-            chunk["z"] = z_t
             chunk["zz"] = zz_t
 
         def slopes(chunk):

@@ -205,7 +205,7 @@ def tile_dendriticlayersilu_ffn_t_v_kernel(tc, x, template_flat, s, grad_out, ou
                             stop=True,
                         )
                         nc.scalar.copy(out=out_sb[:, k0 : k0 + N_MX], in_=acc[:])
-                    nc.scalar.dma_start(out=out_view[:, c * CHUNK + local, w * K : (w + 1) * K], in_=out_sb[:])
+                    nc.sync.dma_start(out=out_view[:, c * CHUNK + local, w * K : (w + 1) * K], in_=out_sb[:])
 
         raw_pieces = [load_template(0), load_template(1)]
         chunks = [load_chunk(0)]

@@ -20,10 +20,7 @@ W = 2
 K = 1024
 N_MX = 512
 ROW_TILES = N_ROWS // P
-CHUNK = 2
-CHUNKS = ROW_TILES // CHUNK
-CW = CHUNK * H
-BRACKET_TO_DS = (-0.25, 0.25)
+TEMPLATE_FACTOR = (0.25, -0.25)
 
 FLOPS = 2 * W * N_ROWS * H * K
 BYTES = 2 * H * W * K + 4 * W * N_ROWS * H + 2 * N_ROWS * H + 4 * N_ROWS * W * K
@@ -40,11 +37,12 @@ def tile_dendriticlayersilu_ffn_t_v_kernel(tc, x, template_flat, s, grad_out, ou
     with ExitStack() as stack:
         const = stack.enter_context(tc.tile_pool(name="const", bufs=1))
         template = stack.enter_context(tc.tile_pool(name="template", bufs=W * K // N_MX))
-        loads = stack.enter_context(tc.tile_pool(name="loads", bufs=4))
-        work = stack.enter_context(tc.tile_pool(name="work", bufs=2))
+        loads = stack.enter_context(tc.tile_pool(name="loads", bufs=5))
+        work = stack.enter_context(tc.tile_pool(name="work", bufs=4))
         turned = stack.enter_context(tc.tile_pool(name="turned", bufs=2))
         stores = stack.enter_context(tc.tile_pool(name="stores", bufs=6))
-        psum_bracket = stack.enter_context(tc.psum_pool(name="psum_bracket", bufs=CHUNK * W))
+        psum_bracket = stack.enter_context(tc.psum_pool(name="psum_bracket", bufs=3))
+        psum_gate = stack.enter_context(tc.psum_pool(name="psum_gate", bufs=1))
         psum_grad = stack.enter_context(tc.psum_pool(name="psum_grad", bufs=1))
         psum_out = stack.enter_context(tc.psum_pool(name="psum_out", bufs=3))
         stack.enter_context(tc.manual_schedule())
@@ -57,16 +55,21 @@ def tile_dendriticlayersilu_ffn_t_v_kernel(tc, x, template_flat, s, grad_out, ou
         template_codes = const.tile([P, W * K], U32, align_bytes=64)
         template_scales = const.tile([P, W * K], U8, align_bytes=64)
 
+        tiles = [{} for t in range(ROW_TILES)]
+
         def load_template(piece):
             raw = template.tile([P, PACK, N_MX], BF16)
             nc.sync.dma_start(out=raw[:], in_=template_view[:, :, piece * N_MX : (piece + 1) * N_MX])
             return raw
 
-        def group_template(raw):
+        def group_template(piece, raw):
             grouped = template.tile([P, N_MX, PACK], BF16, align_bytes=64)
-            nc.vector.tensor_copy(
+            nc.vector.tensor_scalar(
                 out=grouped[:].rearrange("p (c i) j -> p c j i", i=4),
-                in_=raw[:].rearrange("p j (c i) -> p c j i", i=4),
+                in0=raw[:].rearrange("p j (c i) -> p c j i", i=4),
+                scalar1=TEMPLATE_FACTOR[piece * N_MX // K],
+                scalar2=None,
+                op0=ALU.mult,
             )
             return grouped
 
@@ -78,168 +81,203 @@ def tile_dendriticlayersilu_ffn_t_v_kernel(tc, x, template_flat, s, grad_out, ou
                 in_=grouped[:].rearrange("p c j -> p (c j)"),
             )
 
-        def load_chunk(c):
-            tiles = slice(c * CHUNK, (c + 1) * CHUNK)
-            s_sb = loads.tile([P, W, CW], F32)
-            nc.sync.dma_start(out=s_sb[:].rearrange("p w (t h) -> p w t h", h=H), in_=s_view[:, :, tiles, :])
-            g_sb = loads.tile([P, CHUNK, H], BF16)
-            nc.sync.dma_start(out=g_sb[:], in_=g_view[:, tiles, :])
-            chunk = {"s": s_sb, "g": g_sb}
-            window_difference(chunk)
-            return chunk
+        def load_scores(first, count):
+            s_sb = loads.tile([P, W, 2, H], F32)
+            nc.sync.dma_start(out=s_sb[:, :, :count, :], in_=s_view[:, :, first : first + count, :])
+            for i in range(count):
+                tiles[first + i]["s"] = s_sb[:, :, i, :]
 
-        def window_difference(chunk):
-            s_sb = chunk["s"]
-            z_t = work.tile([P, CW], F32, bufs=3)
+        def load_grad(first, count):
+            g_sb = loads.tile([P, 4, H], BF16)
+            nc.sync.dma_start(out=g_sb[:, :count, :], in_=g_view[:, first : first + count, :])
+            for i in range(count):
+                tiles[first + i]["g"] = g_sb[:, i, :]
+
+        def window_difference(t):
+            z_t = work.tile([P, H], F32)
+            s_sb = tiles[t]["s"]
             nc.gpsimd.tensor_tensor(out=z_t[:], in0=s_sb[:, 0, :], in1=s_sb[:, 1, :], op=ALU.subtract)
-            chunk["z"] = z_t
+            tiles[t]["z"] = z_t
 
-        def activations(chunk):
-            s_sb, z_t = chunk["s"], chunk["z"]
-            n_t = work.tile([P, W, CW], F32)
-            f_t = work.tile([P, W, CW], F32)
-            zz_t = work.tile([P, CW], F32)
-            nc.scalar.activation(out=n_t[:], in_=s_sb[:], func=ACT.Tanh, scale=0.5)
-            nc.scalar.activation(out=f_t[:], in_=s_sb[:], func=ACT.Silu)
+        def act_tanh(t):
+            m_t = work.tile([P, W, H], F32)
+            nc.scalar.activation(out=m_t[:], in_=tiles[t]["s"], func=ACT.Tanh, scale=-0.5)
+            tiles[t]["m"] = m_t
+
+        def act_silu(t):
+            f_t = work.tile([P, W, H], F32)
+            nc.scalar.activation(out=f_t[:], in_=tiles[t]["s"], func=ACT.Silu)
+            tiles[t]["f"] = f_t
+
+        def act_gate(t):
+            z_t = tiles[t]["z"]
             nc.scalar.activation(out=z_t[:], in_=z_t[:], func=ACT.Tanh, scale=0.5)
-            nc.scalar.activation(out=zz_t[:], in_=z_t[:], func=ACT.Square)
-            chunk["n"] = n_t
-            chunk["f"] = f_t
-            chunk["zz"] = zz_t
 
-        def slopes(chunk):
-            n_t, f_t = chunk["n"], chunk["f"]
-            shared_t = work.tile([P, CW], F32)
-            nc.vector.scalar_tensor_tensor(
-                out=n_t[:], in0=f_t[:], scalar=1.0, in1=n_t[:], op0=ALU.subtract, op1=ALU.mult
-            )
-            nc.vector.tensor_tensor(out=shared_t[:], in0=f_t[:, 0, :], in1=f_t[:, 1, :], op=ALU.subtract)
-            nc.vector.scalar_tensor_tensor(
-                out=n_t[:], in0=n_t[:], scalar=1.0, in1=f_t[:], op0=ALU.subtract, op1=ALU.subtract
-            )
-            chunk["shared"] = shared_t
+        def silu_difference(t):
+            f_t = tiles[t]["f"]
+            d_t = work.tile([P, H], F32)
+            nc.vector.tensor_tensor(out=d_t[:], in0=f_t[:, 1, :], in1=f_t[:, 0, :], op=ALU.subtract)
+            tiles[t]["d"] = d_t
 
-        def bracket_terms(chunk):
-            n_t, z_t, shared_t = chunk["n"], chunk["z"], chunk["shared"]
-            own_t = work.tile([P, W, CW], F32)
+        def gated_difference(t):
+            k_t = work.tile([P, H], F32)
             nc.vector.scalar_tensor_tensor(
-                out=shared_t[:], in0=chunk["zz"][:], scalar=1.0, in1=shared_t[:], op0=ALU.subtract, op1=ALU.mult
+                out=k_t[:], in0=tiles[t]["z"][:], scalar=1.0, in1=tiles[t]["d"][:], op0=ALU.subtract, op1=ALU.mult
             )
-            nc.vector.scalar_tensor_tensor(
-                out=own_t[:, 0, :], in0=z_t[:], scalar=1.0, in1=n_t[:, 0, :], op0=ALU.add, op1=ALU.mult
-            )
-            nc.vector.scalar_tensor_tensor(
-                out=own_t[:, 1, :], in0=z_t[:], scalar=1.0, in1=n_t[:, 1, :], op0=ALU.subtract, op1=ALU.mult
-            )
-            chunk["own"] = own_t
+            tiles[t]["k"] = k_t
 
-        def turn_grad(chunk):
-            g_ps = psum_grad.tile([P, CHUNK, PACK, P], BF16)
-            for local in range(CHUNK):
-                for j in range(PACK):
-                    nc.tensor.transpose(
-                        out=g_ps[:, local, j, :], in_=chunk["g"][:, local, j * P : (j + 1) * P], identity=ident_bf16[:]
+        def slopes(t):
+            m_t, f_t = tiles[t]["m"], tiles[t]["f"]
+            nc.vector.scalar_tensor_tensor(
+                out=m_t[:], in0=f_t[:], scalar=1.0, in1=m_t[:], op0=ALU.subtract, op1=ALU.mult
+            )
+
+        def turn_grad(t):
+            g_ps = psum_grad.tile([P, PACK, P], BF16)
+            for j in range(PACK):
+                nc.tensor.transpose(out=g_ps[:, j, :], in_=tiles[t]["g"][:, j * P : (j + 1) * P], identity=ident_bf16[:])
+            tiles[t]["g_ps"] = g_ps
+
+        def turn_sum(bank, terms):
+            for j in range(PACK):
+                block = slice(j * P, (j + 1) * P)
+                for i, term in enumerate(terms):
+                    nc.tensor.matmul(
+                        out=bank[:, j, :], lhsT=term[:, block], rhs=ident_f32[:],
+                        is_transpose=True, start=i == 0, stop=i == len(terms) - 1,
                     )
-            chunk["g_ps"] = g_ps
 
-        def turn_brackets(chunk):
-            chunk["brackets"] = []
-            for local in range(CHUNK):
-                for w in range(W):
-                    bracket_ps = psum_bracket.tile([P, PACK, P], F32)
-                    for j in range(PACK):
-                        block = slice(local * H + j * P, local * H + (j + 1) * P)
-                        nc.tensor.matmul(
-                            out=bracket_ps[:, j, :], lhsT=chunk["own"][:, w, block], rhs=ident_f32[:],
-                            is_transpose=True, start=True, stop=False,
-                        )
-                        nc.tensor.matmul(
-                            out=bracket_ps[:, j, :], lhsT=chunk["shared"][:, block], rhs=ident_f32[:],
-                            is_transpose=True, start=False, stop=True,
-                        )
-                    chunk["brackets"].append(bracket_ps)
+        def turn_gate(t):
+            z_ps = psum_gate.tile([P, PACK, P], F32)
+            turn_sum(z_ps, [tiles[t]["z"]])
+            tiles[t]["z_ps"] = z_ps
 
-        def group_grad(chunk):
-            g_turned = turned.tile([P, CHUNK, P, PACK], BF16)
-            nc.scalar.copy(out=g_turned[:], in_=chunk["g_ps"][:].rearrange("p t j m -> p t m j"))
-            chunk["g_turned"] = g_turned
+        def turn_brackets(t):
+            m_t, f_t, k_t, d_t = tiles[t]["m"], tiles[t]["f"], tiles[t]["k"], tiles[t]["d"]
+            tiles[t]["brackets"] = []
+            for w in range(W):
+                bank = psum_bracket.tile([P, PACK, P], F32)
+                terms = [f_t[:, w, :], m_t[:, w, :], k_t]
+                if w == 1:
+                    terms += [d_t, d_t]
+                turn_sum(bank, terms)
+                tiles[t]["brackets"].append(bank)
 
-        def quantise_ds(chunk):
-            ds_bf16 = turned.tile([P, CHUNK, W, P, PACK], BF16, align_bytes=64)
-            ds_codes = turned.tile([P, CHUNK, W * P], U32, align_bytes=64)
-            ds_scales = turned.tile([P, CHUNK, W * P], U8, align_bytes=64)
-            for local in range(CHUNK):
-                for w in range(W):
-                    nc.vector.scalar_tensor_tensor(
-                        out=ds_bf16[:, local, w],
-                        in0=chunk["brackets"][local * W + w][:].rearrange("p j m -> p m j"),
-                        scalar=BRACKET_TO_DS[w],
-                        in1=chunk["g_turned"][:, local],
-                        op0=ALU.mult,
-                        op1=ALU.mult,
-                    )
-            for local in range(CHUNK):
-                nc.vector.quantize_mx(
-                    out=ds_codes[:, local, :].bitcast(E5M2_X4),
-                    scales=ds_scales[:, local, :],
-                    in_=ds_bf16[:, local].rearrange("p w m j -> p (w m j)"),
+        def group_grad(t):
+            g_turned = turned.tile([P, P, PACK], BF16)
+            nc.scalar.copy(out=g_turned[:], in_=tiles[t]["g_ps"][:].rearrange("p j m -> p m j"))
+            tiles[t]["g_turned"] = g_turned
+
+        def gated_grad(t):
+            gg = turned.tile([P, W, P, PACK], F32)
+            for w, op in ((0, ALU.add), (1, ALU.subtract)):
+                nc.vector.scalar_tensor_tensor(
+                    out=gg[:, w], in0=tiles[t]["z_ps"][:].rearrange("p j m -> p m j"), scalar=1.0,
+                    in1=tiles[t]["g_turned"][:], op0=op, op1=ALU.mult,
                 )
-            chunk["ds_codes"] = ds_codes
-            chunk["ds_scales"] = ds_scales
+            tiles[t]["gg"] = gg
 
-        def multiply_and_store(chunk, c):
-            for local in range(CHUNK):
-                for w in range(W):
-                    rows = slice(w * P, (w + 1) * P)
+        def make_ds(t):
+            ds_bf16 = turned.tile([P, W, P, PACK], BF16, align_bytes=64)
+            for w in range(W):
+                nc.vector.scalar_tensor_tensor(
+                    out=ds_bf16[:, w], in0=tiles[t]["brackets"][w][:].rearrange("p j m -> p m j"), scalar=1.0,
+                    in1=tiles[t]["gg"][:, w], op0=ALU.add, op1=ALU.mult,
+                )
+            tiles[t]["ds"] = ds_bf16
+
+        def quantise_ds(t):
+            codes = turned.tile([P, W * P], U32, align_bytes=64)
+            scales = turned.tile([P, W * P], U8, align_bytes=64)
+            nc.vector.quantize_mx(
+                out=codes[:].bitcast(E5M2_X4), scales=scales[:], in_=tiles[t]["ds"][:].rearrange("p w m j -> p (w m j)")
+            )
+            tiles[t]["codes"] = codes
+            tiles[t]["scales"] = scales
+
+        def multiply(t):
+            tiles[t]["acc"] = []
+            for c0 in range(0, W * K, N_MX):
+                rows = slice(c0 // K * P, (c0 // K + 1) * P)
+                cols = slice(c0, c0 + N_MX)
+                acc = psum_out.tile([P, N_MX], F32)
+                nc.tensor.matmul_mx(
+                    out=acc[:],
+                    lhsT=tiles[t]["codes"][:, rows].bitcast(E5M2_X4),
+                    lhsT_scale=tiles[t]["scales"][:, rows],
+                    rhs=template_codes[:, cols].bitcast(E4M3_X4),
+                    rhs_scale=template_scales[:, cols],
+                    start=True,
+                    stop=True,
+                )
+                out_sb = tiles[t].get("out_sb")
+                if c0 % K == 0:
                     out_sb = stores.tile([P, K], F32)
-                    for k0 in range(0, K, N_MX):
-                        cols = slice(w * K + k0, w * K + k0 + N_MX)
-                        acc = psum_out.tile([P, N_MX], F32)
-                        nc.tensor.matmul_mx(
-                            out=acc[:],
-                            lhsT=chunk["ds_codes"][:, local, rows].bitcast(E5M2_X4),
-                            lhsT_scale=chunk["ds_scales"][:, local, rows],
-                            rhs=template_codes[:, cols].bitcast(E4M3_X4),
-                            rhs_scale=template_scales[:, cols],
-                            start=True,
-                            stop=True,
-                        )
-                        nc.scalar.copy(out=out_sb[:, k0 : k0 + N_MX], in_=acc[:])
-                    nc.sync.dma_start(out=out_view[:, c * CHUNK + local, w * K : (w + 1) * K], in_=out_sb[:])
+                    tiles[t]["out_sb"] = out_sb
+                nc.scalar.copy(out=out_sb[:, c0 % K : c0 % K + N_MX], in_=acc[:])
+                if c0 % K + N_MX == K:
+                    nc.sync.dma_start(out=out_view[:, t, c0 // K * K : c0 // K * K + K], in_=out_sb[:])
 
-        raw_pieces = [load_template(0), load_template(1)]
-        chunks = [load_chunk(0)]
+        load_scores(0, 1)
+        raw_pieces = [load_template(0)]
+        load_grad(0, 4)
+        load_scores(1, 1)
+        raw_pieces.append(load_template(1))
         raw_pieces.append(load_template(2))
+        load_scores(2, 2)
         raw_pieces.append(load_template(3))
-        chunks.append(load_chunk(1))
-        chunks.append(load_chunk(2))
+        load_scores(4, 2)
+        load_grad(4, 4)
+        load_scores(6, 2)
 
-        grouped_pieces = [group_template(raw_pieces[0]), group_template(raw_pieces[1])]
-        quantise_template(0, grouped_pieces[0])
-        activations(chunks[0])
-        quantise_template(1, grouped_pieces[1])
-        grouped_pieces.append(group_template(raw_pieces[2]))
-        grouped_pieces.append(group_template(raw_pieces[3]))
-        quantise_template(2, grouped_pieces[2])
-        activations(chunks[1])
-        quantise_template(3, grouped_pieces[3])
-        turn_grad(chunks[0])
-        group_grad(chunks[0])
-        slopes(chunks[0])
-        bracket_terms(chunks[0])
+        for t in range(3):
+            window_difference(t)
+        for t in range(2):
+            act_tanh(t)
+            act_silu(t)
+            act_gate(t)
+        grouped = [group_template(0, raw_pieces[0]), group_template(1, raw_pieces[1])]
+        silu_difference(0)
+        quantise_template(0, grouped[0])
+        gated_difference(0)
+        slopes(0)
+        quantise_template(1, grouped[1])
+        grouped.append(group_template(2, raw_pieces[2]))
+        grouped.append(group_template(3, raw_pieces[3]))
+        quantise_template(2, grouped[2])
+        turn_grad(0)
+        turn_gate(0)
+        turn_brackets(0)
 
-        for c in range(CHUNKS):
-            if c + 3 < CHUNKS:
-                chunks.append(load_chunk(c + 3))
-            turn_brackets(chunks[c])
-            if c + 1 < CHUNKS:
-                turn_grad(chunks[c + 1])
-            if c + 2 < CHUNKS:
-                activations(chunks[c + 2])
-            if c + 1 < CHUNKS:
-                group_grad(chunks[c + 1])
-                slopes(chunks[c + 1])
-            quantise_ds(chunks[c])
-            multiply_and_store(chunks[c], c)
-            if c + 1 < CHUNKS:
-                bracket_terms(chunks[c + 1])
+        for t in range(ROW_TILES + 1):
+            if t + 3 < ROW_TILES:
+                window_difference(t + 3)
+            if t % 2 == 0 and t + 8 < ROW_TILES:
+                load_scores(t + 8, 2)
+            if t % 4 == 0 and t + 8 < ROW_TILES:
+                load_grad(t + 8, 4)
+            if t + 2 < ROW_TILES:
+                act_tanh(t + 2)
+            if t < ROW_TILES:
+                group_grad(t)
+            if t + 1 < ROW_TILES:
+                silu_difference(t + 1)
+            if t == 0:
+                quantise_template(3, grouped[3])
+            if t > 0:
+                quantise_ds(t - 1)
+                multiply(t - 1)
+            if t + 1 < ROW_TILES:
+                turn_grad(t + 1)
+                gated_difference(t + 1)
+                slopes(t + 1)
+                turn_brackets(t + 1)
+            if t < ROW_TILES:
+                gated_grad(t)
+            if t + 1 < ROW_TILES:
+                turn_gate(t + 1)
+            if t + 2 < ROW_TILES:
+                act_silu(t + 2)
+                act_gate(t + 2)
+            if t < ROW_TILES:
+                make_ds(t)

@@ -38,8 +38,8 @@ def tile_dendriticlayersilu_ffn_t_v_kernel(tc, x, template_flat, s, grad_out, ou
         const = stack.enter_context(tc.tile_pool(name="const", bufs=1))
         template = stack.enter_context(tc.tile_pool(name="template", bufs=W * K // N_MX))
         loads = stack.enter_context(tc.tile_pool(name="loads", bufs=5))
-        work = stack.enter_context(tc.tile_pool(name="work", bufs=4))
-        turned = stack.enter_context(tc.tile_pool(name="turned", bufs=2))
+        work = stack.enter_context(tc.tile_pool(name="work", bufs=6))
+        turned = stack.enter_context(tc.tile_pool(name="turned", bufs=3))
         stores = stack.enter_context(tc.tile_pool(name="stores", bufs=6))
         psum_bracket = stack.enter_context(tc.psum_pool(name="psum_bracket", bufs=3))
         psum_gate = stack.enter_context(tc.psum_pool(name="psum_gate", bufs=1))
@@ -152,39 +152,33 @@ def tile_dendriticlayersilu_ffn_t_v_kernel(tc, x, template_flat, s, grad_out, ou
             turn_sum(z_ps, [tiles[t]["z"]])
             tiles[t]["z_ps"] = z_ps
 
-        def turn_brackets(t):
-            m_t, f_t, k_t, d_t = tiles[t]["m"], tiles[t]["f"], tiles[t]["k"], tiles[t]["d"]
-            tiles[t]["brackets"] = []
-            for w in range(W):
-                bank = psum_bracket.tile([P, PACK, P], F32)
-                terms = [f_t[:, w, :], m_t[:, w, :], k_t]
-                if w == 1:
-                    terms += [d_t, d_t]
-                turn_sum(bank, terms)
-                tiles[t]["brackets"].append(bank)
+        def turn_bracket(t, w):
+            bank = psum_bracket.tile([P, PACK, P], F32)
+            turn_sum(bank, [tiles[t]["f"][:, w, :], tiles[t]["k"]] + [tiles[t]["d"]] * (2 * w) + [tiles[t]["m"][:, w, :]])
+            tiles[t][w] = bank
 
         def group_grad(t):
             g_turned = turned.tile([P, P, PACK], BF16)
             nc.scalar.copy(out=g_turned[:], in_=tiles[t]["g_ps"][:].rearrange("p j m -> p m j"))
             tiles[t]["g_turned"] = g_turned
 
-        def gated_grad(t):
-            gg = turned.tile([P, W, P, PACK], F32)
-            for w, op in ((0, ALU.add), (1, ALU.subtract)):
-                nc.vector.scalar_tensor_tensor(
-                    out=gg[:, w], in0=tiles[t]["z_ps"][:].rearrange("p j m -> p m j"), scalar=1.0,
-                    in1=tiles[t]["g_turned"][:], op0=op, op1=ALU.mult,
-                )
-            tiles[t]["gg"] = gg
+        def gated_grad(t, w):
+            if w == 0:
+                gg = turned.tile([P, W, P, PACK], F32)
+                tiles[t]["gg"] = gg
+            nc.vector.scalar_tensor_tensor(
+                out=tiles[t]["gg"][:, w], in0=tiles[t]["z_ps"][:].rearrange("p j m -> p m j"), scalar=1.0,
+                in1=tiles[t]["g_turned"][:], op0=(ALU.add, ALU.subtract)[w], op1=ALU.mult,
+            )
 
-        def make_ds(t):
-            ds_bf16 = turned.tile([P, W, P, PACK], BF16, align_bytes=64)
-            for w in range(W):
-                nc.vector.scalar_tensor_tensor(
-                    out=ds_bf16[:, w], in0=tiles[t]["brackets"][w][:].rearrange("p j m -> p m j"), scalar=1.0,
-                    in1=tiles[t]["gg"][:, w], op0=ALU.add, op1=ALU.mult,
-                )
-            tiles[t]["ds"] = ds_bf16
+        def make_ds(t, w):
+            if w == 0:
+                ds_bf16 = turned.tile([P, W, P, PACK], BF16, align_bytes=64)
+                tiles[t]["ds"] = ds_bf16
+            nc.vector.scalar_tensor_tensor(
+                out=tiles[t]["ds"][:, w], in0=tiles[t][w][:].rearrange("p j m -> p m j"), scalar=1.0,
+                in1=tiles[t]["gg"][:, w], op0=ALU.add, op1=ALU.mult,
+            )
 
         def quantise_ds(t):
             codes = turned.tile([P, W * P], U32, align_bytes=64)
@@ -195,89 +189,88 @@ def tile_dendriticlayersilu_ffn_t_v_kernel(tc, x, template_flat, s, grad_out, ou
             tiles[t]["codes"] = codes
             tiles[t]["scales"] = scales
 
-        def multiply(t):
-            tiles[t]["acc"] = []
-            for c0 in range(0, W * K, N_MX):
-                rows = slice(c0 // K * P, (c0 // K + 1) * P)
-                cols = slice(c0, c0 + N_MX)
-                acc = psum_out.tile([P, N_MX], F32)
-                nc.tensor.matmul_mx(
-                    out=acc[:],
-                    lhsT=tiles[t]["codes"][:, rows].bitcast(E5M2_X4),
-                    lhsT_scale=tiles[t]["scales"][:, rows],
-                    rhs=template_codes[:, cols].bitcast(E4M3_X4),
-                    rhs_scale=template_scales[:, cols],
-                    start=True,
-                    stop=True,
-                )
-                out_sb = tiles[t].get("out_sb")
-                if c0 % K == 0:
-                    out_sb = stores.tile([P, K], F32)
-                    tiles[t]["out_sb"] = out_sb
-                nc.scalar.copy(out=out_sb[:, c0 % K : c0 % K + N_MX], in_=acc[:])
-                if c0 % K + N_MX == K:
-                    nc.sync.dma_start(out=out_view[:, t, c0 // K * K : c0 // K * K + K], in_=out_sb[:])
+        def multiply(t, c0):
+            rows = slice(c0 // K * P, (c0 // K + 1) * P)
+            acc = psum_out.tile([P, N_MX], F32)
+            nc.tensor.matmul_mx(
+                out=acc[:],
+                lhsT=tiles[t]["codes"][:, rows].bitcast(E5M2_X4),
+                lhsT_scale=tiles[t]["scales"][:, rows],
+                rhs=template_codes[:, c0 : c0 + N_MX].bitcast(E4M3_X4),
+                rhs_scale=template_scales[:, c0 : c0 + N_MX],
+                start=True,
+                stop=True,
+            )
+            tiles[t]["acc", c0] = acc
+
+        def store(t, c0):
+            if c0 % K == 0:
+                out_sb = stores.tile([P, K], F32)
+                tiles[t]["out_sb"] = out_sb
+            out_sb = tiles[t]["out_sb"]
+            nc.scalar.copy(out=out_sb[:, c0 % K : c0 % K + N_MX], in_=tiles[t]["acc", c0][:])
+            if c0 % K + N_MX == K:
+                nc.sync.dma_start(out=out_view[:, t, c0 // K * K : c0 // K * K + K], in_=out_sb[:])
 
         load_scores(0, 1)
-        raw_pieces = [load_template(0)]
+        raw = [load_template(0)]
         load_grad(0, 4)
         load_scores(1, 1)
-        raw_pieces.append(load_template(1))
-        raw_pieces.append(load_template(2))
+        raw.append(load_template(1))
+        raw.append(load_template(2))
         load_scores(2, 2)
-        raw_pieces.append(load_template(3))
-        load_scores(4, 2)
-        load_grad(4, 4)
-        load_scores(6, 2)
+        raw.append(load_template(3))
 
-        for t in range(3):
-            window_difference(t)
-        for t in range(2):
-            act_tanh(t)
-            act_silu(t)
-            act_gate(t)
-        grouped = [group_template(0, raw_pieces[0]), group_template(1, raw_pieces[1])]
-        silu_difference(0)
-        quantise_template(0, grouped[0])
-        gated_difference(0)
-        slopes(0)
-        quantise_template(1, grouped[1])
-        grouped.append(group_template(2, raw_pieces[2]))
-        grouped.append(group_template(3, raw_pieces[3]))
-        quantise_template(2, grouped[2])
-        turn_grad(0)
-        turn_gate(0)
-        turn_brackets(0)
+        def at(t, step, *args):
+            if 0 <= t < ROW_TILES:
+                step(t, *args)
 
-        for t in range(ROW_TILES + 1):
-            if t + 3 < ROW_TILES:
-                window_difference(t + 3)
-            if t % 2 == 0 and t + 8 < ROW_TILES:
-                load_scores(t + 8, 2)
-            if t % 4 == 0 and t + 8 < ROW_TILES:
-                load_grad(t + 8, 4)
-            if t + 2 < ROW_TILES:
-                act_tanh(t + 2)
-            if t < ROW_TILES:
-                group_grad(t)
-            if t + 1 < ROW_TILES:
-                silu_difference(t + 1)
-            if t == 0:
-                quantise_template(3, grouped[3])
-            if t > 0:
-                quantise_ds(t - 1)
-                multiply(t - 1)
-            if t + 1 < ROW_TILES:
-                turn_grad(t + 1)
-                gated_difference(t + 1)
-                slopes(t + 1)
-                turn_brackets(t + 1)
-            if t < ROW_TILES:
-                gated_grad(t)
-            if t + 1 < ROW_TILES:
-                turn_gate(t + 1)
-            if t + 2 < ROW_TILES:
-                act_silu(t + 2)
-                act_gate(t + 2)
-            if t < ROW_TILES:
-                make_ds(t)
+        grouped = []
+        template_steps = [
+            lambda: grouped.append(group_template(0, raw[0])),
+            lambda: grouped.append(group_template(1, raw[1])),
+            lambda: quantise_template(0, grouped[0]),
+            lambda: quantise_template(1, grouped[1]),
+            lambda: grouped.append(group_template(2, raw[2])),
+            lambda: grouped.append(group_template(3, raw[3])),
+            lambda: quantise_template(2, grouped[2]),
+            lambda: quantise_template(3, grouped[3]),
+        ]
+
+        def template_step():
+            if template_steps:
+                template_steps.pop(0)()
+
+        for t in range(-4, ROW_TILES + 1):
+            if t + 8 < ROW_TILES:
+                if t % 2 == 0 and t + 8 > 3:
+                    load_scores(t + 8, 2)
+                if t % 4 == 0 and t + 8 > 3:
+                    load_grad(t + 8, 4)
+            at(t + 4, window_difference)
+            at(t + 1, group_grad)
+            at(t + 3, act_tanh)
+            at(t, gated_grad, 0)
+            at(t - 1, quantise_ds)
+            at(t + 1, turn_bracket, 0)
+            at(t - 1, multiply, 0)
+            at(t - 1, multiply, N_MX)
+            at(t - 1, multiply, K)
+            at(t - 1, multiply, K + N_MX)
+            at(t + 2, turn_grad)
+            at(t - 1, store, 0)
+            at(t - 1, store, N_MX)
+            at(t - 1, store, K)
+            at(t - 1, store, K + N_MX)
+            at(t, gated_grad, 1)
+            at(t + 2, silu_difference)
+            template_step()
+            at(t, make_ds, 0)
+            at(t + 1, turn_gate)
+            at(t + 1, turn_bracket, 1)
+            at(t + 2, gated_difference)
+            at(t, make_ds, 1)
+            at(t + 3, act_silu)
+            at(t + 2, slopes)
+            template_step()
+            at(t + 3, act_gate)

@@ -37,14 +37,13 @@ def tile_dendriticlayersilu_ffn_t_v_kernel(tc, x, template_flat, s, grad_out, ou
     with ExitStack() as stack:
         const = stack.enter_context(tc.tile_pool(name="const", bufs=1))
         template = stack.enter_context(tc.tile_pool(name="template", bufs=W * K // N_MX))
-        loads = stack.enter_context(tc.tile_pool(name="loads", bufs=5))
+        loads = stack.enter_context(tc.tile_pool(name="loads", bufs=4))
         work = stack.enter_context(tc.tile_pool(name="work", bufs=6))
         turned = stack.enter_context(tc.tile_pool(name="turned", bufs=3))
         stores = stack.enter_context(tc.tile_pool(name="stores", bufs=6))
         psum_bracket = stack.enter_context(tc.psum_pool(name="psum_bracket", bufs=3))
         psum_gate = stack.enter_context(tc.psum_pool(name="psum_gate", bufs=1))
-        psum_grad = stack.enter_context(tc.psum_pool(name="psum_grad", bufs=1))
-        psum_out = stack.enter_context(tc.psum_pool(name="psum_out", bufs=3))
+        psum_out = stack.enter_context(tc.psum_pool(name="psum_out", bufs=4))
         stack.enter_context(tc.manual_schedule())
 
         ident_f32 = const.tile([P, P], F32)
@@ -94,10 +93,10 @@ def tile_dendriticlayersilu_ffn_t_v_kernel(tc, x, template_flat, s, grad_out, ou
                 tiles[first + i]["g"] = g_sb[:, i, :]
 
         def window_difference(t):
-            z_t = work.tile([P, H], F32)
             s_sb = tiles[t]["s"]
-            nc.gpsimd.tensor_tensor(out=z_t[:], in0=s_sb[:, 0, :], in1=s_sb[:, 1, :], op=ALU.subtract)
-            tiles[t]["z"] = z_t
+            diff = turned.tile([P, H], F32, tag="difference_or_ds", bufs=3, align_bytes=64)
+            nc.gpsimd.tensor_tensor(out=diff[:], in0=s_sb[:, 0, :], in1=s_sb[:, 1, :], op=ALU.subtract)
+            tiles[t]["diff"] = diff
 
         def act_tanh(t):
             m_t = work.tile([P, W, H], F32)
@@ -110,13 +109,14 @@ def tile_dendriticlayersilu_ffn_t_v_kernel(tc, x, template_flat, s, grad_out, ou
             tiles[t]["f"] = f_t
 
         def act_gate(t):
-            z_t = tiles[t]["z"]
-            nc.scalar.activation(out=z_t[:], in_=z_t[:], func=ACT.Tanh, scale=0.5)
+            z_t = work.tile([P, H], F32)
+            nc.scalar.activation(out=z_t[:], in_=tiles[t]["diff"][:], func=ACT.Tanh, scale=0.5)
+            tiles[t]["z"] = z_t
 
         def silu_difference(t):
             f_t = tiles[t]["f"]
             d_t = work.tile([P, H], F32)
-            nc.vector.tensor_tensor(out=d_t[:], in0=f_t[:, 1, :], in1=f_t[:, 0, :], op=ALU.subtract)
+            nc.gpsimd.tensor_tensor(out=d_t[:], in0=f_t[:, 1, :], in1=f_t[:, 0, :], op=ALU.subtract)
             tiles[t]["d"] = d_t
 
         def gated_difference(t):
@@ -126,6 +126,13 @@ def tile_dendriticlayersilu_ffn_t_v_kernel(tc, x, template_flat, s, grad_out, ou
             )
             tiles[t]["k"] = k_t
 
+        def other_gated_difference(t):
+            l_t = work.tile([P, H], F32)
+            nc.vector.scalar_tensor_tensor(
+                out=l_t[:], in0=tiles[t]["z"][:], scalar=1.0, in1=tiles[t]["d"][:], op0=ALU.add, op1=ALU.mult
+            )
+            tiles[t]["l"] = l_t
+
         def slopes(t):
             m_t, f_t = tiles[t]["m"], tiles[t]["f"]
             nc.vector.scalar_tensor_tensor(
@@ -133,7 +140,7 @@ def tile_dendriticlayersilu_ffn_t_v_kernel(tc, x, template_flat, s, grad_out, ou
             )
 
         def turn_grad(t):
-            g_ps = psum_grad.tile([P, PACK, P], BF16)
+            g_ps = psum_out.tile([P, PACK, P], BF16, tag="grad_or_product")
             for j in range(PACK):
                 nc.tensor.transpose(out=g_ps[:, j, :], in_=tiles[t]["g"][:, j * P : (j + 1) * P], identity=ident_bf16[:])
             tiles[t]["g_ps"] = g_ps
@@ -154,7 +161,7 @@ def tile_dendriticlayersilu_ffn_t_v_kernel(tc, x, template_flat, s, grad_out, ou
 
         def turn_bracket(t, w):
             bank = psum_bracket.tile([P, PACK, P], F32)
-            turn_sum(bank, [tiles[t]["f"][:, w, :], tiles[t]["k"]] + [tiles[t]["d"]] * (2 * w) + [tiles[t]["m"][:, w, :]])
+            turn_sum(bank, [tiles[t]["f"][:, w, :], tiles[t]["m"][:, w, :], tiles[t][("k", "l")[w]]])
             tiles[t][w] = bank
 
         def group_grad(t):
@@ -173,7 +180,7 @@ def tile_dendriticlayersilu_ffn_t_v_kernel(tc, x, template_flat, s, grad_out, ou
 
         def make_ds(t, w):
             if w == 0:
-                ds_bf16 = turned.tile([P, W, P, PACK], BF16, align_bytes=64)
+                ds_bf16 = turned.tile([P, W, P, PACK], BF16, tag="difference_or_ds", bufs=3, align_bytes=64)
                 tiles[t]["ds"] = ds_bf16
             nc.vector.scalar_tensor_tensor(
                 out=tiles[t]["ds"][:, w], in0=tiles[t][w][:].rearrange("p j m -> p m j"), scalar=1.0,
@@ -191,7 +198,7 @@ def tile_dendriticlayersilu_ffn_t_v_kernel(tc, x, template_flat, s, grad_out, ou
 
         def multiply(t, c0):
             rows = slice(c0 // K * P, (c0 // K + 1) * P)
-            acc = psum_out.tile([P, N_MX], F32)
+            acc = psum_out.tile([P, N_MX], F32, tag="grad_or_product")
             nc.tensor.matmul_mx(
                 out=acc[:],
                 lhsT=tiles[t]["codes"][:, rows].bitcast(E5M2_X4),
@@ -241,36 +248,37 @@ def tile_dendriticlayersilu_ffn_t_v_kernel(tc, x, template_flat, s, grad_out, ou
             if template_steps:
                 template_steps.pop(0)()
 
-        for t in range(-4, ROW_TILES + 1):
+        for t in range(-4, ROW_TILES + 2):
             if t + 8 < ROW_TILES:
                 if t % 2 == 0 and t + 8 > 3:
                     load_scores(t + 8, 2)
                 if t % 4 == 0 and t + 8 > 3:
                     load_grad(t + 8, 4)
-            at(t + 4, window_difference)
             at(t + 1, group_grad)
             at(t + 3, act_tanh)
             at(t, gated_grad, 0)
-            at(t - 1, quantise_ds)
+            at(t, gated_grad, 1)
+            template_step()
             at(t + 1, turn_bracket, 0)
             at(t - 1, multiply, 0)
             at(t - 1, multiply, N_MX)
             at(t - 1, multiply, K)
             at(t - 1, multiply, K + N_MX)
             at(t + 2, turn_grad)
+            at(t + 1, turn_gate)
             at(t - 1, store, 0)
             at(t - 1, store, N_MX)
             at(t - 1, store, K)
             at(t - 1, store, K + N_MX)
-            at(t, gated_grad, 1)
-            at(t + 2, silu_difference)
-            template_step()
-            at(t, make_ds, 0)
-            at(t + 1, turn_gate)
-            at(t + 1, turn_bracket, 1)
-            at(t + 2, gated_difference)
-            at(t, make_ds, 1)
             at(t + 3, act_silu)
+            at(t + 3, act_gate)
+            at(t, make_ds, 0)
+            at(t + 4, window_difference)
+            at(t + 2, silu_difference)
+            at(t, make_ds, 1)
+            at(t + 1, turn_bracket, 1)
             at(t + 2, slopes)
             template_step()
-            at(t + 3, act_gate)
+            at(t + 2, gated_difference)
+            at(t + 2, other_gated_difference)
+            at(t, quantise_ds)

@@ -37,7 +37,7 @@ def tile_dendriticlayersilu_ffn_t_v_kernel(tc, x, template_flat, s, grad_out, ou
     with ExitStack() as stack:
         const = stack.enter_context(tc.tile_pool(name="const", bufs=1))
         template = stack.enter_context(tc.tile_pool(name="template", bufs=W * K // N_MX))
-        loads = stack.enter_context(tc.tile_pool(name="loads", bufs=4))
+        loads = stack.enter_context(tc.tile_pool(name="loads", bufs=5))
         work = stack.enter_context(tc.tile_pool(name="work", bufs=6))
         turned = stack.enter_context(tc.tile_pool(name="turned", bufs=3))
         stores = stack.enter_context(tc.tile_pool(name="stores", bufs=6))
@@ -126,13 +126,6 @@ def tile_dendriticlayersilu_ffn_t_v_kernel(tc, x, template_flat, s, grad_out, ou
             )
             tiles[t]["k"] = k_t
 
-        def other_gated_difference(t):
-            l_t = work.tile([P, H], F32)
-            nc.vector.scalar_tensor_tensor(
-                out=l_t[:], in0=tiles[t]["z"][:], scalar=1.0, in1=tiles[t]["d"][:], op0=ALU.add, op1=ALU.mult
-            )
-            tiles[t]["l"] = l_t
-
         def slopes(t):
             m_t, f_t = tiles[t]["m"], tiles[t]["f"]
             nc.vector.scalar_tensor_tensor(
@@ -161,7 +154,7 @@ def tile_dendriticlayersilu_ffn_t_v_kernel(tc, x, template_flat, s, grad_out, ou
 
         def turn_bracket(t, w):
             bank = psum_bracket.tile([P, PACK, P], F32)
-            turn_sum(bank, [tiles[t]["f"][:, w, :], tiles[t]["m"][:, w, :], tiles[t][("k", "l")[w]]])
+            turn_sum(bank, [tiles[t]["f"][:, w, :], tiles[t]["k"]] + [tiles[t]["d"]] * (2 * w) + [tiles[t]["m"][:, w, :]])
             tiles[t][w] = bank
 
         def group_grad(t):
@@ -215,7 +208,11 @@ def tile_dendriticlayersilu_ffn_t_v_kernel(tc, x, template_flat, s, grad_out, ou
                 out_sb = stores.tile([P, K], F32)
                 tiles[t]["out_sb"] = out_sb
             out_sb = tiles[t]["out_sb"]
-            nc.scalar.copy(out=out_sb[:, c0 % K : c0 % K + N_MX], in_=tiles[t]["acc", c0][:])
+            dst, acc = out_sb[:, c0 % K : c0 % K + N_MX], tiles[t]["acc", c0]
+            if c0 == K + N_MX or (t == ROW_TILES - 1 and c0 == N_MX):
+                nc.vector.tensor_copy(out=dst, in_=acc[:])
+            else:
+                nc.scalar.copy(out=dst, in_=acc[:])
             if c0 % K + N_MX == K:
                 nc.sync.dma_start(out=out_view[:, t, c0 // K * K : c0 // K * K + K], in_=out_sb[:])
 
@@ -254,11 +251,12 @@ def tile_dendriticlayersilu_ffn_t_v_kernel(tc, x, template_flat, s, grad_out, ou
                     load_scores(t + 8, 2)
                 if t % 4 == 0 and t + 8 > 3:
                     load_grad(t + 8, 4)
-            at(t + 1, group_grad)
             at(t + 3, act_tanh)
+            at(t + 1, group_grad)
             at(t, gated_grad, 0)
             at(t, gated_grad, 1)
             template_step()
+            at(t - 2, store, K + N_MX)
             at(t + 1, turn_bracket, 0)
             at(t - 1, multiply, 0)
             at(t - 1, multiply, N_MX)
@@ -269,7 +267,6 @@ def tile_dendriticlayersilu_ffn_t_v_kernel(tc, x, template_flat, s, grad_out, ou
             at(t - 1, store, 0)
             at(t - 1, store, N_MX)
             at(t - 1, store, K)
-            at(t - 1, store, K + N_MX)
             at(t + 3, act_silu)
             at(t + 3, act_gate)
             at(t, make_ds, 0)
@@ -280,5 +277,4 @@ def tile_dendriticlayersilu_ffn_t_v_kernel(tc, x, template_flat, s, grad_out, ou
             at(t + 2, slopes)
             template_step()
             at(t + 2, gated_difference)
-            at(t + 2, other_gated_difference)
             at(t, quantise_ds)

from contextlib import ExitStack

import concourse.mybir as mybir
from concourse.masks import make_identity

F32 = mybir.dt.float32
BF16 = mybir.dt.bfloat16
U32 = mybir.dt.uint32
U8 = mybir.dt.uint8
E5M2_X4 = mybir.dt.float8_e5m2_x4
E4M3_X4 = mybir.dt.float8_e4m3fn_x4
ALU = mybir.AluOpType
ACT = mybir.ActivationFunctionType

P = 128
PACK = 4
N_ROWS = 2048
H = P * PACK
W = 2
K = 1024
N_MX = 512
ROW_TILES = N_ROWS // P
TEMPLATE_FACTOR = (0.25, -0.25)

FLOPS = 2 * W * N_ROWS * H * K
BYTES = 2 * H * W * K + 4 * W * N_ROWS * H + 2 * N_ROWS * H + 4 * N_ROWS * W * K


def tile_dendriticlayersilu_ffn_t_v_kernel(tc, x, template_flat, s, grad_out, out):
    nc = tc.nc

    s_view = s.rearrange("w (p t) h -> p w t h", t=ROW_TILES)
    g_view = grad_out.rearrange("(p t) h -> p t h", t=ROW_TILES)
    out_view = out.rearrange("(p t) c -> p t c", t=ROW_TILES)
    template_view = template_flat.rearrange("(j p) c -> p j c", p=P)

    with ExitStack() as stack:
        const = stack.enter_context(tc.tile_pool(name="const", bufs=1))
        template = stack.enter_context(tc.tile_pool(name="template", bufs=W * K // N_MX))
        loads = stack.enter_context(tc.tile_pool(name="loads", bufs=5))
        work = stack.enter_context(tc.tile_pool(name="work", bufs=6))
        turned = stack.enter_context(tc.tile_pool(name="turned", bufs=3))
        stores = stack.enter_context(tc.tile_pool(name="stores", bufs=6))
        psum_bracket = stack.enter_context(tc.psum_pool(name="psum_bracket", bufs=3))
        psum_gate = stack.enter_context(tc.psum_pool(name="psum_gate", bufs=1))
        psum_out = stack.enter_context(tc.psum_pool(name="psum_out", bufs=4))
        stack.enter_context(tc.manual_schedule())

        ident_f32 = const.tile([P, P], F32)
        make_identity(nc, ident_f32[:])
        ident_bf16 = const.tile([P, P], BF16)
        make_identity(nc, ident_bf16[:])

        template_codes = const.tile([P, W * K], U32, align_bytes=64)
        template_scales = const.tile([P, W * K], U8, align_bytes=64)

        tiles = [{} for t in range(ROW_TILES)]

        def load_template(piece):
            raw = template.tile([P, PACK, N_MX], BF16)
            nc.sync.dma_start(out=raw[:], in_=template_view[:, :, piece * N_MX : (piece + 1) * N_MX])
            return raw

        def group_template(piece, raw):
            grouped = template.tile([P, N_MX, PACK], BF16, align_bytes=64)
            nc.vector.tensor_scalar(
                out=grouped[:].rearrange("p (c i) j -> p c j i", i=4),
                in0=raw[:].rearrange("p j (c i) -> p c j i", i=4),
                scalar1=TEMPLATE_FACTOR[piece * N_MX // K],
                scalar2=None,
                op0=ALU.mult,
            )
            return grouped

        def quantise_template(piece, grouped):
            cols = slice(piece * N_MX, (piece + 1) * N_MX)
            nc.vector.quantize_mx(
                out=template_codes[:, cols].bitcast(E4M3_X4),
                scales=template_scales[:, cols],
                in_=grouped[:].rearrange("p c j -> p (c j)"),
            )

        def load_scores(first, count):
            s_sb = loads.tile([P, W, 2, H], F32)
            nc.sync.dma_start(out=s_sb[:, :, :count, :], in_=s_view[:, :, first : first + count, :])
            for i in range(count):
                tiles[first + i]["s"] = s_sb[:, :, i, :]

        def load_grad(first, count):
            g_sb = loads.tile([P, 4, H], BF16)
            nc.sync.dma_start(out=g_sb[:, :count, :], in_=g_view[:, first : first + count, :])
            for i in range(count):
                tiles[first + i]["g"] = g_sb[:, i, :]

        def window_difference(t):
            s_sb = tiles[t]["s"]
            diff = turned.tile([P, H], F32, tag="difference_or_ds", bufs=3, align_bytes=64)
            nc.gpsimd.tensor_tensor(out=diff[:], in0=s_sb[:, 0, :], in1=s_sb[:, 1, :], op=ALU.subtract)
            tiles[t]["diff"] = diff

        def act_tanh(t):
            m_t = work.tile([P, W, H], F32)
            nc.scalar.activation(out=m_t[:], in_=tiles[t]["s"], func=ACT.Tanh, scale=-0.5)
            tiles[t]["m"] = m_t

        def act_silu(t):
            f_t = work.tile([P, W, H], F32)
            nc.scalar.activation(out=f_t[:], in_=tiles[t]["s"], func=ACT.Silu)
            tiles[t]["f"] = f_t

        def act_gate(t):
            z_t = work.tile([P, H], F32)
            nc.scalar.activation(out=z_t[:], in_=tiles[t]["diff"][:], func=ACT.Tanh, scale=0.5)
            tiles[t]["z"] = z_t

        def silu_difference(t):
            f_t = tiles[t]["f"]
            d_t = work.tile([P, H], F32)
            nc.gpsimd.tensor_tensor(out=d_t[:], in0=f_t[:, 1, :], in1=f_t[:, 0, :], op=ALU.subtract)
            tiles[t]["d"] = d_t

        def gated_difference(t):
            k_t = work.tile([P, H], F32)
            nc.vector.scalar_tensor_tensor(
                out=k_t[:], in0=tiles[t]["z"][:], scalar=1.0, in1=tiles[t]["d"][:], op0=ALU.subtract, op1=ALU.mult
            )
            tiles[t]["k"] = k_t

        def slopes(t):
            m_t, f_t = tiles[t]["m"], tiles[t]["f"]
            nc.vector.scalar_tensor_tensor(
                out=m_t[:], in0=f_t[:], scalar=1.0, in1=m_t[:], op0=ALU.subtract, op1=ALU.mult
            )

        def turn_grad(t):
            g_ps = psum_out.tile([P, PACK, P], BF16, tag="grad_or_product")
            for j in range(PACK):
                nc.tensor.transpose(out=g_ps[:, j, :], in_=tiles[t]["g"][:, j * P : (j + 1) * P], identity=ident_bf16[:])
            tiles[t]["g_ps"] = g_ps

        def turn_sum(bank, terms):
            for j in range(PACK):
                block = slice(j * P, (j + 1) * P)
                for i, term in enumerate(terms):
                    nc.tensor.matmul(
                        out=bank[:, j, :], lhsT=term[:, block], rhs=ident_f32[:],
                        is_transpose=True, start=i == 0, stop=i == len(terms) - 1,
                    )

        def turn_gate(t):
            z_ps = psum_gate.tile([P, PACK, P], F32)
            turn_sum(z_ps, [tiles[t]["z"]])
            tiles[t]["z_ps"] = z_ps

        def turn_bracket(t, w):
            bank = psum_bracket.tile([P, PACK, P], F32)
            turn_sum(bank, [tiles[t]["f"][:, w, :], tiles[t]["k"]] + [tiles[t]["d"]] * (2 * w) + [tiles[t]["m"][:, w, :]])
            tiles[t][w] = bank

        def group_grad(t):
            g_turned = turned.tile([P, P, PACK], BF16)
            nc.scalar.copy(out=g_turned[:], in_=tiles[t]["g_ps"][:].rearrange("p j m -> p m j"))
            tiles[t]["g_turned"] = g_turned

        def gated_grad(t, w):
            if w == 0:
                gg = turned.tile([P, W, P, PACK], F32)
                tiles[t]["gg"] = gg
            nc.vector.scalar_tensor_tensor(
                out=tiles[t]["gg"][:, w], in0=tiles[t]["z_ps"][:].rearrange("p j m -> p m j"), scalar=1.0,
                in1=tiles[t]["g_turned"][:], op0=(ALU.add, ALU.subtract)[w], op1=ALU.mult,
            )

        def make_ds(t, w):
            if w == 0:
                ds_bf16 = turned.tile([P, W, P, PACK], BF16, tag="difference_or_ds", bufs=3, align_bytes=64)
                tiles[t]["ds"] = ds_bf16
            nc.vector.scalar_tensor_tensor(
                out=tiles[t]["ds"][:, w], in0=tiles[t][w][:].rearrange("p j m -> p m j"), scalar=1.0,
                in1=tiles[t]["gg"][:, w], op0=ALU.add, op1=ALU.mult,
            )

        def quantise_ds(t):
            codes = turned.tile([P, W * P], U32, align_bytes=64)
            scales = turned.tile([P, W * P], U8, align_bytes=64)
            nc.vector.quantize_mx(
                out=codes[:].bitcast(E5M2_X4), scales=scales[:], in_=tiles[t]["ds"][:].rearrange("p w m j -> p (w m j)")
            )
            tiles[t]["codes"] = codes
            tiles[t]["scales"] = scales

        def multiply(t, c0):
            rows = slice(c0 // K * P, (c0 // K + 1) * P)
            acc = psum_out.tile([P, N_MX], F32, tag="grad_or_product")
            nc.tensor.matmul_mx(
                out=acc[:],
                lhsT=tiles[t]["codes"][:, rows].bitcast(E5M2_X4),
                lhsT_scale=tiles[t]["scales"][:, rows],
                rhs=template_codes[:, c0 : c0 + N_MX].bitcast(E4M3_X4),
                rhs_scale=template_scales[:, c0 : c0 + N_MX],
                start=True,
                stop=True,
            )
            tiles[t]["acc", c0] = acc

        def store(t, c0):
            if c0 % K == 0:
                out_sb = stores.tile([P, K], F32)
                tiles[t]["out_sb"] = out_sb
            out_sb = tiles[t]["out_sb"]
            dst, acc = out_sb[:, c0 % K : c0 % K + N_MX], tiles[t]["acc", c0]
            if c0 == K + N_MX or (t == ROW_TILES - 1 and c0 == N_MX):
                nc.vector.tensor_copy(out=dst, in_=acc[:])
            else:
                nc.scalar.copy(out=dst, in_=acc[:])
            if c0 % K + N_MX == K:
                nc.sync.dma_start(out=out_view[:, t, c0 // K * K : c0 // K * K + K], in_=out_sb[:])

        load_scores(0, 1)
        raw = [load_template(0)]
        load_grad(0, 4)
        load_scores(1, 1)
        raw.append(load_template(1))
        raw.append(load_template(2))
        load_scores(2, 2)
        raw.append(load_template(3))

        def at(t, step, *args):
            if 0 <= t < ROW_TILES:
                step(t, *args)

        grouped = []
        template_steps = [
            lambda: grouped.append(group_template(0, raw[0])),
            lambda: grouped.append(group_template(1, raw[1])),
            lambda: quantise_template(0, grouped[0]),
            lambda: quantise_template(1, grouped[1]),
            lambda: grouped.append(group_template(2, raw[2])),
            lambda: grouped.append(group_template(3, raw[3])),
            lambda: quantise_template(2, grouped[2]),
            lambda: quantise_template(3, grouped[3]),
        ]

        def template_step():
            if template_steps:
                template_steps.pop(0)()

        for t in range(-4, ROW_TILES + 2):
            if t + 8 < ROW_TILES:
                if t % 2 == 0 and t + 8 > 3:
                    load_scores(t + 8, 2)
                if t % 4 == 0 and t + 8 > 3:
                    load_grad(t + 8, 4)
            at(t + 3, act_tanh)
            at(t + 1, group_grad)
            at(t, gated_grad, 0)
            at(t, gated_grad, 1)
            template_step()
            at(t - 2, store, K + N_MX)
            at(t + 1, turn_bracket, 0)
            at(t - 1, multiply, 0)
            at(t - 1, multiply, N_MX)
            at(t - 1, multiply, K)
            at(t - 1, multiply, K + N_MX)
            at(t + 2, turn_grad)
            at(t + 1, turn_gate)
            at(t - 1, store, 0)
            at(t - 1, store, N_MX)
            at(t - 1, store, K)
            at(t + 3, act_silu)
            at(t + 3, act_gate)
            at(t, make_ds, 0)
            at(t + 4, window_difference)
            at(t + 2, silu_difference)
            at(t, make_ds, 1)
            at(t + 1, turn_bracket, 1)
            at(t + 2, slopes)
            template_step()
            at(t + 2, gated_difference)
            at(t, quantise_ds)
